import numpy as np
import ml_dtypes


def mxq(x, axis, fmt="e4m3"):
    dtype, down = {"e4m3": (ml_dtypes.float8_e4m3fn, 7), "e5m2": (ml_dtypes.float8_e5m2, 14)}[fmt]
    v = np.moveaxis(np.asarray(x, np.float32).astype(ml_dtypes.bfloat16).astype(np.float64), axis, -1)
    blocks = v.reshape(v.shape[:-1] + (-1, 32))
    amax = np.abs(blocks).max(-1, keepdims=True)
    byte = np.maximum(np.where(amax > 0, np.frexp(amax)[1] - 1 + 127, 0) - down, 1)
    scale = np.exp2(byte - 127.0)
    codes = (blocks / scale).astype(np.float32).astype(dtype).astype(np.float64)
    return np.moveaxis((codes * scale).reshape(v.shape), -1, axis)


WIDE = False


def mx_kscale(k):
    if not WIDE:
        return np.ones(k)
    levels = np.array([10, -10, 5, -5, 0])
    a = np.random.permutation(np.resize(levels, k // 512 * 4)).reshape(k // 512, 4)
    idx = np.arange(k)
    return np.exp2(a[idx // 512, idx % 128 // 32])


BF16 = ml_dtypes.bfloat16


def bf(x):
    return np.asarray(x, np.float32).astype(BF16)


def f64(x):
    return np.asarray(x).astype(np.float64)


B, T, D, H, DH, F = 4, 256, 1024, 16, 64, 4096
A = H * DH
EPS = 1e-6


def layer_norm(v, gain, bias):
    mu = v.mean(-1, keepdims=True)
    var = np.square(v - mu).mean(-1, keepdims=True)
    return (v - mu) * (1.0 / np.sqrt(var + EPS)) * gain + bias


def setup_inputs():
    s = mx_kscale(D)
    r = np.random.standard_normal
    return {"x": bf(r((B, T, D))),
            "ln1_gain": bf((1.0 + 0.1 * r(D)) * s),
            "ln1_bias": bf(0.1 * r(D) * s),
            "wq": bf(r((D, A)) / np.sqrt(D) / s[:, None]),
            "bq": bf(0.1 * r(A)),
            "wk": bf(r((D, A)) / np.sqrt(D) / s[:, None]),
            "bk": bf(0.1 * r(A)),
            "wv": bf(r((D, A)) / np.sqrt(D) / s[:, None]),
            "bv": bf(0.1 * r(A))}


def reference(x, ln1_gain, ln1_bias, wq, bq, wk, bk, wv, bv):
    h = layer_norm(f64(x), f64(ln1_gain), f64(ln1_bias))
    hq = mxq(h, 2, "e4m3")
    q = ((hq @ mxq(f64(wq), 0, "e4m3")) + f64(bq)).reshape(B, T, H, DH)
    k = ((hq @ mxq(f64(wk), 0, "e4m3")) + f64(bk)).reshape(B, T, H, DH)
    v = ((hq @ mxq(f64(wv), 0, "e4m3")) + f64(bv)).reshape(B, T, H, DH)
    return q, k, v

@@ -1,0 +1,246 @@
+from contextlib import ExitStack
+
+import concourse.mybir as mybir
+from concourse.masks import make_identity
+
+F32 = mybir.dt.float32
+BF16 = mybir.dt.bfloat16
+U32 = mybir.dt.uint32
+U8 = mybir.dt.uint8
+FP8X4 = mybir.dt.float8_e4m3fn_x4
+ALU = mybir.AluOpType
+ACT = mybir.ActivationFunctionType
+
+P = 128
+PACK = 4
+K_PASS = P * PACK
+D = 1024
+PASSES = D // K_PASS
+CHUNKS = D // P
+TOKENS = 1024
+TOKEN_TILES = TOKENS // P
+HALF_TILES = TOKEN_TILES // 2
+HALF_TOKENS = HALF_TILES * P
+WIDTH = 1024
+N_BLOCK = 512
+BLOCKS_PER_WEIGHT = WIDTH // N_BLOCK
+BLOCKS = 3 * BLOCKS_PER_WEIGHT
+STAT_PIECE = 512
+RUN = 4
+EPS = 1e-6
+
+FLOPS = 2 * TOKENS * D * 3 * WIDTH
+
+
+def regroup(copy, grouped, rows):
+    copy(
+        out=grouped.rearrange("p (c i) t -> p c t i", i=RUN),
+        in_=rows.rearrange("p t (c i) -> p c t i", i=RUN),
+    )
+
+
+def tile_swidtblock_pa_kernel(
+    tc, x, ln1_gain, ln1_bias, wq, bq, wk, bk, wv, bv, out_0, out_1, out_2
+):
+    nc = tc.nc
+    x_rows = x.flatten_outer_dims()
+    weights = [wq, wk, wv]
+    biases = [bq, bk, bv]
+    outs = [o.rearrange("b t h e -> (b t) (h e)") for o in (out_0, out_1, out_2)]
+
+    with ExitStack() as ctx:
+        keep = ctx.enter_context(tc.tile_pool(name="keep", bufs=1))
+        h_stage = ctx.enter_context(tc.tile_pool(name="h_stage", bufs=2))
+        w_stage = ctx.enter_context(tc.tile_pool(name="w_stage", bufs=4))
+        o_stage = ctx.enter_context(tc.tile_pool(name="o_stage", bufs=6))
+        psum = ctx.enter_context(tc.psum_pool(name="psum", bufs=4))
+
+        ident_f32 = keep.tile([P, P], F32)
+        make_identity(nc, ident_f32[:])
+        ident_bf = keep.tile([P, P], BF16)
+        nc.vector.tensor_copy(out=ident_bf[:], in_=ident_f32[:])
+        eps_t = keep.tile([P, 1], F32)
+        nc.vector.memset(eps_t[:], EPS)
+        warm = keep.tile([P, 1], F32)
+        nc.scalar.activation(out=warm[:], in_=eps_t[:], func=ACT.Sqrt)
+
+        norm_rows = keep.tile([P, P], BF16)
+        nc.vector.memset(norm_rows[:], 0.0)
+        nc.scalar.dma_start(out=norm_rows[0:CHUNKS, :], in_=ln1_gain.rearrange("(r c) -> r c", c=P))
+        nc.scalar.dma_start(
+            out=norm_rows[CHUNKS : 2 * CHUNKS, :], in_=ln1_bias.rearrange("(r c) -> r c", c=P)
+        )
+        bias_rows = keep.tile([P, N_BLOCK], BF16)
+        nc.vector.memset(bias_rows[:], 0.0)
+        for w in range(3):
+            nc.scalar.dma_start(
+                out=bias_rows[BLOCKS_PER_WEIGHT * w : BLOCKS_PER_WEIGHT * (w + 1), :],
+                in_=biases[w].rearrange("(r c) -> r c", c=N_BLOCK),
+            )
+
+        x_sb = keep.tile([P, TOKEN_TILES, D], BF16)
+        w_raw = keep.tile([P, 3, PASSES, PACK, WIDTH], BF16)
+
+        def load_x(i):
+            nc.sync.dma_start(out=x_sb[:, i, :], in_=x_rows[P * i : P * (i + 1), :])
+
+        def load_w(w, g):
+            view = weights[w].rearrange("(g t p) n -> g p t n", t=PACK, p=P)
+            nc.sync.dma_start(out=w_raw[:, w, g, :, :], in_=view[g])
+
+        for i in range(HALF_TILES):
+            load_x(i)
+        load_w(0, 0)
+        for i in range(HALF_TILES, TOKEN_TILES):
+            load_x(i)
+        load_w(0, 1)
+        for w in range(1, 3):
+            for g in range(PASSES):
+                load_w(w, g)
+
+        norm_ps = psum.tile([P, N_BLOCK], F32, tag="acc")
+        nc.tensor.matmul(
+            out=norm_ps[:, 0:P], lhsT=norm_rows[:], rhs=ident_bf[:], start=True, stop=True
+        )
+        norm_cols = keep.tile([P, 2 * CHUNKS], F32)
+        nc.scalar.copy(out=norm_cols[:], in_=norm_ps[:, 0 : 2 * CHUNKS])
+        bias_all = keep.tile([P, BLOCKS * N_BLOCK], F32)
+        for b in range(BLOCKS):
+            bias_ps = psum.tile([P, N_BLOCK], F32, tag="acc")
+            nc.tensor.matmul(
+                out=bias_ps[:],
+                lhsT=ident_bf[:, b : b + 1].to_broadcast([P, P]),
+                rhs=bias_rows[:],
+                start=True,
+                stop=True,
+            )
+            nc.scalar.copy(out=bias_all[:, N_BLOCK * b : N_BLOCK * (b + 1)], in_=bias_ps[:])
+
+        stats = keep.tile([P, TOKEN_TILES, D // STAT_PIECE, 6], F32)
+        mean_var = keep.tile([P, TOKEN_TILES, 2], F32)
+        std = keep.tile([P, TOKEN_TILES], F32)
+        rstd = keep.tile([P, TOKEN_TILES], F32)
+        shift = keep.tile([P, TOKEN_TILES], F32)
+        normed = keep.tile([P, TOKEN_TILES, D], F32)
+
+        def normalise(i):
+            for c in range(D // STAT_PIECE):
+                nc.vector.bn_stats(
+                    out=stats[:, i, c, :], in_=x_sb[:, i, STAT_PIECE * c : STAT_PIECE * (c + 1)]
+                )
+            nc.vector.bn_aggr(
+                out=mean_var[:, i, :], in_=stats[:, i, :, :].rearrange("p c s -> p (c s)")
+            )
+            nc.scalar.activation(
+                out=std[:, i : i + 1], in_=mean_var[:, i, 1:2], func=ACT.Sqrt, bias=eps_t[:, 0:1]
+            )
+            nc.vector.reciprocal(out=rstd[:, i : i + 1], in_=std[:, i : i + 1])
+            nc.vector.tensor_scalar(
+                out=shift[:, i : i + 1],
+                in0=mean_var[:, i, 0:1],
+                scalar1=rstd[:, i : i + 1],
+                scalar2=-1.0,
+                op0=ALU.mult,
+                op1=ALU.mult,
+            )
+            nc.gpsimd.tensor_scalar(
+                out=normed[:, i, :],
+                in0=x_sb[:, i, :],
+                scalar1=rstd[:, i : i + 1],
+                scalar2=shift[:, i : i + 1],
+                op0=ALU.mult,
+                op1=ALU.add,
+            )
+
+        h_rows = keep.tile([P, 2, CHUNKS, HALF_TOKENS], BF16)
+        h_codes = keep.tile([P, PASSES, TOKENS], U32, align_bytes=64)
+        h_scales = keep.tile([P, PASSES, TOKENS], U8, align_bytes=64)
+
+        def transpose_and_scale(half):
+            for j in range(CHUNKS):
+                turned = psum.tile([P, HALF_TOKENS], F32, tag="turned")
+                for s in range(HALF_TILES):
+                    nc.tensor.transpose(
+                        turned[:, P * s : P * (s + 1)],
+                        normed[:, HALF_TILES * half + s, P * j : P * (j + 1)],
+                        ident_f32[:],
+                    )
+                nc.scalar.activation(
+                    out=h_rows[:, half, j, :],
+                    in_=turned[:],
+                    func=ACT.Identity,
+                    bias=norm_cols[:, CHUNKS + j : CHUNKS + j + 1],
+                    scale=norm_cols[:, j : j + 1],
+                )
+
+        def quantise_h(half):
+            tokens = slice(HALF_TOKENS * half, HALF_TOKENS * (half + 1))
+            for g in range(PASSES):
+                grouped_h = h_stage.tile([P, HALF_TOKENS, PACK], BF16, align_bytes=64)
+                regroup(nc.vector.tensor_copy, grouped_h[:], h_rows[:, half, PACK * g : PACK * (g + 1), :])
+                nc.vector.quantize_mx(
+                    out=h_codes[:, g, tokens].bitcast(FP8X4),
+                    scales=h_scales[:, g, tokens],
+                    in_=grouped_h[:].rearrange("p r t -> p (r t)"),
+                )
+
+        w_codes = keep.tile([P, PASSES, BLOCKS * N_BLOCK], U32, align_bytes=64)
+        w_scales = keep.tile([P, PASSES, BLOCKS * N_BLOCK], U8, align_bytes=64)
+
+        def regroup_w(b, g):
+            w, part = divmod(b, BLOCKS_PER_WEIGHT)
+            grouped_w = w_stage.tile([P, N_BLOCK, PACK], BF16, align_bytes=64)
+            regroup(
+                nc.scalar.copy, grouped_w[:], w_raw[:, w, g, :, N_BLOCK * part : N_BLOCK * (part + 1)]
+            )
+            return grouped_w
+
+        def quantise_w(b, g, grouped_w):
+            cols = slice(N_BLOCK * b, N_BLOCK * (b + 1))
+            nc.vector.quantize_mx(
+                out=w_codes[:, g, cols].bitcast(FP8X4),
+                scales=w_scales[:, g, cols],
+                in_=grouped_w[:].rearrange("p c t -> p (c t)"),
+            )
+
+        def project(b, i):
+            w, part = divmod(b, BLOCKS_PER_WEIGHT)
+            cols = slice(N_BLOCK * b, N_BLOCK * (b + 1))
+            tokens = slice(P * i, P * (i + 1))
+            acc = psum.tile([P, N_BLOCK], F32, tag="acc")
+            for g in range(PASSES):
+                nc.tensor.matmul_mx(
+                    out=acc[:],
+                    lhsT=h_codes[:, g, tokens].bitcast(FP8X4),
+                    lhsT_scale=h_scales[:, g, tokens],
+                    rhs=w_codes[:, g, cols].bitcast(FP8X4),
+                    rhs_scale=w_scales[:, g, cols],
+                    start=(g == 0),
+                    stop=(g == PASSES - 1),
+                )
+            result = o_stage.tile([P, N_BLOCK], F32)
+            nc.vector.tensor_tensor(out=result[:], in0=acc[:], in1=bias_all[:, cols], op=ALU.add)
+            nc.sync.dma_start(
+                out=outs[w][tokens, N_BLOCK * part : N_BLOCK * (part + 1)], in_=result[:]
+            )
+
+        for i in range(HALF_TILES):
+            normalise(i)
+        first_0 = regroup_w(0, 0)
+        for i in range(HALF_TILES, TOKEN_TILES):
+            normalise(i)
+        transpose_and_scale(0)
+        first_1 = regroup_w(0, 1)
+        quantise_h(0)
+        quantise_w(0, 0, first_0)
+        quantise_w(0, 1, first_1)
+        transpose_and_scale(1)
+        quantise_h(1)
+        for b in range(BLOCKS):
+            for g in range(PASSES):
+                if b + 1 < BLOCKS:
+                    grouped_next = regroup_w(b + 1, g)
+                for i in range(HALF_TILES * g, HALF_TILES * (g + 1)):
+                    project(b, i)
+                if b + 1 < BLOCKS:
+                    quantise_w(b + 1, g, grouped_next)

@@ -28,6 +28,7 @@ BLOCKS = 3 * BLOCKS_PER_WEIGHT
 STAT_PIECE = 512
 RUN = 4
 EPS = 1e-6
+SCALAR_SHARE = 4
 
 FLOPS = 2 * TOKENS * D * 3 * WIDTH
 
@@ -52,28 +53,28 @@ def tile_swidtblock_pa_kernel(
         keep = ctx.enter_context(tc.tile_pool(name="keep", bufs=1))
         h_stage = ctx.enter_context(tc.tile_pool(name="h_stage", bufs=2))
         w_stage = ctx.enter_context(tc.tile_pool(name="w_stage", bufs=4))
-        o_stage = ctx.enter_context(tc.tile_pool(name="o_stage", bufs=6))
-        psum = ctx.enter_context(tc.psum_pool(name="psum", bufs=4))
+        o_stage = ctx.enter_context(tc.tile_pool(name="o_stage", bufs=8))
+        psum = ctx.enter_context(tc.psum_pool(name="psum", bufs=8))
 
-        ident_f32 = keep.tile([P, P], F32)
-        make_identity(nc, ident_f32[:])
-        ident_bf = keep.tile([P, P], BF16)
-        nc.vector.tensor_copy(out=ident_bf[:], in_=ident_f32[:])
         eps_t = keep.tile([P, 1], F32)
         nc.vector.memset(eps_t[:], EPS)
         warm = keep.tile([P, 1], F32)
         nc.scalar.activation(out=warm[:], in_=eps_t[:], func=ACT.Sqrt)
+        ident_f32 = keep.tile([P, P], F32)
+        make_identity(nc, ident_f32[:])
+        ident_bf = keep.tile([P, P], BF16)
+        nc.vector.tensor_copy(out=ident_bf[:], in_=ident_f32[:])
 
         norm_rows = keep.tile([P, P], BF16)
         nc.vector.memset(norm_rows[:], 0.0)
-        nc.scalar.dma_start(out=norm_rows[0:CHUNKS, :], in_=ln1_gain.rearrange("(r c) -> r c", c=P))
-        nc.scalar.dma_start(
+        nc.sync.dma_start(out=norm_rows[0:CHUNKS, :], in_=ln1_gain.rearrange("(r c) -> r c", c=P))
+        nc.sync.dma_start(
             out=norm_rows[CHUNKS : 2 * CHUNKS, :], in_=ln1_bias.rearrange("(r c) -> r c", c=P)
         )
         bias_rows = keep.tile([P, N_BLOCK], BF16)
         nc.vector.memset(bias_rows[:], 0.0)
         for w in range(3):
-            nc.scalar.dma_start(
+            nc.sync.dma_start(
                 out=bias_rows[BLOCKS_PER_WEIGHT * w : BLOCKS_PER_WEIGHT * (w + 1), :],
                 in_=biases[w].rearrange("(r c) -> r c", c=N_BLOCK),
             )
@@ -98,7 +99,7 @@ def tile_swidtblock_pa_kernel(
             for g in range(PASSES):
                 load_w(w, g)
 
-        norm_ps = psum.tile([P, N_BLOCK], F32, tag="acc")
+        norm_ps = psum.tile([P, N_BLOCK], F32, tag="bank")
         nc.tensor.matmul(
             out=norm_ps[:, 0:P], lhsT=norm_rows[:], rhs=ident_bf[:], start=True, stop=True
         )
@@ -106,7 +107,7 @@ def tile_swidtblock_pa_kernel(
         nc.scalar.copy(out=norm_cols[:], in_=norm_ps[:, 0 : 2 * CHUNKS])
         bias_all = keep.tile([P, BLOCKS * N_BLOCK], F32)
         for b in range(BLOCKS):
-            bias_ps = psum.tile([P, N_BLOCK], F32, tag="acc")
+            bias_ps = psum.tile([P, N_BLOCK], F32, tag="bank")
             nc.tensor.matmul(
                 out=bias_ps[:],
                 lhsT=ident_bf[:, b : b + 1].to_broadcast([P, P]),
@@ -123,7 +124,7 @@ def tile_swidtblock_pa_kernel(
         shift = keep.tile([P, TOKEN_TILES], F32)
         normed = keep.tile([P, TOKEN_TILES, D], F32)
 
-        def normalise(i):
+        def statistics(i):
             for c in range(D // STAT_PIECE):
                 nc.vector.bn_stats(
                     out=stats[:, i, c, :], in_=x_sb[:, i, STAT_PIECE * c : STAT_PIECE * (c + 1)]
@@ -131,18 +132,26 @@ def tile_swidtblock_pa_kernel(
             nc.vector.bn_aggr(
                 out=mean_var[:, i, :], in_=stats[:, i, :, :].rearrange("p c s -> p (c s)")
             )
+
+        def root(half):
+            tiles = slice(HALF_TILES * half, HALF_TILES * (half + 1))
             nc.scalar.activation(
-                out=std[:, i : i + 1], in_=mean_var[:, i, 1:2], func=ACT.Sqrt, bias=eps_t[:, 0:1]
+                out=std[:, tiles], in_=mean_var[:, tiles, 1], func=ACT.Sqrt, bias=eps_t[:, 0:1]
             )
-            nc.vector.reciprocal(out=rstd[:, i : i + 1], in_=std[:, i : i + 1])
-            nc.vector.tensor_scalar(
-                out=shift[:, i : i + 1],
-                in0=mean_var[:, i, 0:1],
-                scalar1=rstd[:, i : i + 1],
-                scalar2=-1.0,
+
+        def scale_and_shift(half):
+            tiles = slice(HALF_TILES * half, HALF_TILES * (half + 1))
+            nc.vector.reciprocal(out=rstd[:, tiles], in_=std[:, tiles])
+            nc.vector.scalar_tensor_tensor(
+                out=shift[:, tiles],
+                in0=mean_var[:, tiles, 0],
+                scalar=-1.0,
+                in1=rstd[:, tiles],
                 op0=ALU.mult,
                 op1=ALU.mult,
             )
+
+        def normalise(i):
             nc.gpsimd.tensor_scalar(
                 out=normed[:, i, :],
                 in0=x_sb[:, i, :],
@@ -158,7 +167,7 @@ def tile_swidtblock_pa_kernel(
 
         def transpose_and_scale(half):
             for j in range(CHUNKS):
-                turned = psum.tile([P, HALF_TOKENS], F32, tag="turned")
+                turned = psum.tile([P, HALF_TOKENS], F32, tag="bank")
                 for s in range(HALF_TILES):
                     nc.tensor.transpose(
                         turned[:, P * s : P * (s + 1)],
@@ -173,26 +182,28 @@ def tile_swidtblock_pa_kernel(
                     scale=norm_cols[:, j : j + 1],
                 )
 
-        def quantise_h(half):
+        def regroup_h(half, g):
+            grouped_h = h_stage.tile([P, HALF_TOKENS, PACK], BF16, align_bytes=64)
+            regroup(
+                nc.vector.tensor_copy, grouped_h[:], h_rows[:, half, PACK * g : PACK * (g + 1), :]
+            )
+            return grouped_h
+
+        def quantise_h(half, g, grouped_h):
             tokens = slice(HALF_TOKENS * half, HALF_TOKENS * (half + 1))
-            for g in range(PASSES):
-                grouped_h = h_stage.tile([P, HALF_TOKENS, PACK], BF16, align_bytes=64)
-                regroup(nc.vector.tensor_copy, grouped_h[:], h_rows[:, half, PACK * g : PACK * (g + 1), :])
-                nc.vector.quantize_mx(
-                    out=h_codes[:, g, tokens].bitcast(FP8X4),
-                    scales=h_scales[:, g, tokens],
-                    in_=grouped_h[:].rearrange("p r t -> p (r t)"),
-                )
+            nc.vector.quantize_mx(
+                out=h_codes[:, g, tokens].bitcast(FP8X4),
+                scales=h_scales[:, g, tokens],
+                in_=grouped_h[:].rearrange("p r t -> p (r t)"),
+            )
 
         w_codes = keep.tile([P, PASSES, BLOCKS * N_BLOCK], U32, align_bytes=64)
         w_scales = keep.tile([P, PASSES, BLOCKS * N_BLOCK], U8, align_bytes=64)
 
-        def regroup_w(b, g):
+        def regroup_w(copy, b, g):
             w, part = divmod(b, BLOCKS_PER_WEIGHT)
             grouped_w = w_stage.tile([P, N_BLOCK, PACK], BF16, align_bytes=64)
-            regroup(
-                nc.scalar.copy, grouped_w[:], w_raw[:, w, g, :, N_BLOCK * part : N_BLOCK * (part + 1)]
-            )
+            regroup(copy, grouped_w[:], w_raw[:, w, g, :, N_BLOCK * part : N_BLOCK * (part + 1)])
             return grouped_w
 
         def quantise_w(b, g, grouped_w):
@@ -207,7 +218,7 @@ def tile_swidtblock_pa_kernel(
             w, part = divmod(b, BLOCKS_PER_WEIGHT)
             cols = slice(N_BLOCK * b, N_BLOCK * (b + 1))
             tokens = slice(P * i, P * (i + 1))
-            acc = psum.tile([P, N_BLOCK], F32, tag="acc")
+            acc = psum.tile([P, N_BLOCK], F32, tag="bank")
             for g in range(PASSES):
                 nc.tensor.matmul_mx(
                     out=acc[:],
@@ -219,28 +230,66 @@ def tile_swidtblock_pa_kernel(
                     stop=(g == PASSES - 1),
                 )
             result = o_stage.tile([P, N_BLOCK], F32)
-            nc.vector.tensor_tensor(out=result[:], in0=acc[:], in1=bias_all[:, cols], op=ALU.add)
+            if i % SCALAR_SHARE == SCALAR_SHARE - 1:
+                nc.scalar.copy(out=result[:], in_=acc[:])
+                nc.gpsimd.tensor_tensor(
+                    out=result[:], in0=result[:], in1=bias_all[:, cols], op=ALU.add
+                )
+            else:
+                nc.vector.tensor_tensor(
+                    out=result[:], in0=acc[:], in1=bias_all[:, cols], op=ALU.add
+                )
             nc.sync.dma_start(
                 out=outs[w][tokens, N_BLOCK * part : N_BLOCK * (part + 1)], in_=result[:]
             )
 
+        def project_half(b, half):
+            for i in range(HALF_TILES * half, HALF_TILES * (half + 1)):
+                project(b, i)
+
+        for i in range(HALF_TILES):
+            statistics(i)
+        root(0)
+        statistics(HALF_TILES)
+        scale_and_shift(0)
         for i in range(HALF_TILES):
             normalise(i)
-        first_0 = regroup_w(0, 0)
+        w00 = regroup_w(nc.scalar.copy, 0, 0)
+        w10 = regroup_w(nc.scalar.copy, 1, 0)
+        for i in range(HALF_TILES + 1, TOKEN_TILES):
+            statistics(i)
+        root(1)
+        w01 = regroup_w(nc.vector.tensor_copy, 0, 1)
+        scale_and_shift(1)
         for i in range(HALF_TILES, TOKEN_TILES):
             normalise(i)
+        w11 = regroup_w(nc.vector.tensor_copy, 1, 1)
+        quantise_w(0, 0, w00)
+        quantise_w(1, 0, w10)
+        quantise_w(0, 1, w01)
+        quantise_w(1, 1, w11)
         transpose_and_scale(0)
-        first_1 = regroup_w(0, 1)
-        quantise_h(0)
-        quantise_w(0, 0, first_0)
-        quantise_w(0, 1, first_1)
+        h00 = regroup_h(0, 0)
+        quantise_h(0, 0, h00)
+        h01 = regroup_h(0, 1)
         transpose_and_scale(1)
-        quantise_h(1)
-        for b in range(BLOCKS):
+        quantise_h(0, 1, h01)
+        project_half(0, 0)
+        h10 = regroup_h(1, 0)
+        project_half(1, 0)
+        h11 = regroup_h(1, 1)
+        quantise_h(1, 0, h10)
+        quantise_h(1, 1, h11)
+        w20 = regroup_w(nc.scalar.copy, 2, 0)
+        project_half(0, 1)
+        quantise_w(2, 0, w20)
+        w21 = regroup_w(nc.scalar.copy, 2, 1)
+        project_half(1, 1)
+        quantise_w(2, 1, w21)
+        for b in range(2, BLOCKS):
             for g in range(PASSES):
                 if b + 1 < BLOCKS:
-                    grouped_next = regroup_w(b + 1, g)
-                for i in range(HALF_TILES * g, HALF_TILES * (g + 1)):
-                    project(b, i)
+                    grouped_next = regroup_w(nc.scalar.copy, b + 1, g)
+                project_half(b, g)
                 if b + 1 < BLOCKS:
                     quantise_w(b + 1, g, grouped_next)

@@ -54,27 +54,27 @@ def tile_swidtblock_pa_kernel(
         h_stage = ctx.enter_context(tc.tile_pool(name="h_stage", bufs=2))
         w_stage = ctx.enter_context(tc.tile_pool(name="w_stage", bufs=4))
         o_stage = ctx.enter_context(tc.tile_pool(name="o_stage", bufs=8))
-        psum = ctx.enter_context(tc.psum_pool(name="psum", bufs=8))
+        psum = ctx.enter_context(tc.psum_pool(name="psum", bufs=4))
 
-        eps_t = keep.tile([P, 1], F32)
-        nc.vector.memset(eps_t[:], EPS)
-        warm = keep.tile([P, 1], F32)
-        nc.scalar.activation(out=warm[:], in_=eps_t[:], func=ACT.Sqrt)
         ident_f32 = keep.tile([P, P], F32)
         make_identity(nc, ident_f32[:])
         ident_bf = keep.tile([P, P], BF16)
         nc.vector.tensor_copy(out=ident_bf[:], in_=ident_f32[:])
+        eps_t = keep.tile([P, 1], F32)
+        nc.vector.memset(eps_t[:], EPS)
+        warm = keep.tile([P, 1], F32)
+        nc.scalar.activation(out=warm[:], in_=eps_t[:], func=ACT.Sqrt)
 
         norm_rows = keep.tile([P, P], BF16)
         nc.vector.memset(norm_rows[:], 0.0)
-        nc.sync.dma_start(out=norm_rows[0:CHUNKS, :], in_=ln1_gain.rearrange("(r c) -> r c", c=P))
-        nc.sync.dma_start(
+        nc.scalar.dma_start(out=norm_rows[0:CHUNKS, :], in_=ln1_gain.rearrange("(r c) -> r c", c=P))
+        nc.scalar.dma_start(
             out=norm_rows[CHUNKS : 2 * CHUNKS, :], in_=ln1_bias.rearrange("(r c) -> r c", c=P)
         )
         bias_rows = keep.tile([P, N_BLOCK], BF16)
         nc.vector.memset(bias_rows[:], 0.0)
         for w in range(3):
-            nc.sync.dma_start(
+            nc.scalar.dma_start(
                 out=bias_rows[BLOCKS_PER_WEIGHT * w : BLOCKS_PER_WEIGHT * (w + 1), :],
                 in_=biases[w].rearrange("(r c) -> r c", c=N_BLOCK),
             )
@@ -99,7 +99,7 @@ def tile_swidtblock_pa_kernel(
             for g in range(PASSES):
                 load_w(w, g)
 
-        norm_ps = psum.tile([P, N_BLOCK], F32, tag="bank")
+        norm_ps = psum.tile([P, N_BLOCK], F32, tag="acc")
         nc.tensor.matmul(
             out=norm_ps[:, 0:P], lhsT=norm_rows[:], rhs=ident_bf[:], start=True, stop=True
         )
@@ -107,7 +107,7 @@ def tile_swidtblock_pa_kernel(
         nc.scalar.copy(out=norm_cols[:], in_=norm_ps[:, 0 : 2 * CHUNKS])
         bias_all = keep.tile([P, BLOCKS * N_BLOCK], F32)
         for b in range(BLOCKS):
-            bias_ps = psum.tile([P, N_BLOCK], F32, tag="bank")
+            bias_ps = psum.tile([P, N_BLOCK], F32, tag="acc")
             nc.tensor.matmul(
                 out=bias_ps[:],
                 lhsT=ident_bf[:, b : b + 1].to_broadcast([P, P]),
@@ -124,7 +124,7 @@ def tile_swidtblock_pa_kernel(
         shift = keep.tile([P, TOKEN_TILES], F32)
         normed = keep.tile([P, TOKEN_TILES, D], F32)
 
-        def statistics(i):
+        def normalise(i):
             for c in range(D // STAT_PIECE):
                 nc.vector.bn_stats(
                     out=stats[:, i, c, :], in_=x_sb[:, i, STAT_PIECE * c : STAT_PIECE * (c + 1)]
@@ -132,26 +132,18 @@ def tile_swidtblock_pa_kernel(
             nc.vector.bn_aggr(
                 out=mean_var[:, i, :], in_=stats[:, i, :, :].rearrange("p c s -> p (c s)")
             )
-
-        def root(half):
-            tiles = slice(HALF_TILES * half, HALF_TILES * (half + 1))
             nc.scalar.activation(
-                out=std[:, tiles], in_=mean_var[:, tiles, 1], func=ACT.Sqrt, bias=eps_t[:, 0:1]
+                out=std[:, i : i + 1], in_=mean_var[:, i, 1:2], func=ACT.Sqrt, bias=eps_t[:, 0:1]
             )
-
-        def scale_and_shift(half):
-            tiles = slice(HALF_TILES * half, HALF_TILES * (half + 1))
-            nc.vector.reciprocal(out=rstd[:, tiles], in_=std[:, tiles])
-            nc.vector.scalar_tensor_tensor(
-                out=shift[:, tiles],
-                in0=mean_var[:, tiles, 0],
-                scalar=-1.0,
-                in1=rstd[:, tiles],
+            nc.vector.reciprocal(out=rstd[:, i : i + 1], in_=std[:, i : i + 1])
+            nc.vector.tensor_scalar(
+                out=shift[:, i : i + 1],
+                in0=mean_var[:, i, 0:1],
+                scalar1=rstd[:, i : i + 1],
+                scalar2=-1.0,
                 op0=ALU.mult,
                 op1=ALU.mult,
             )
-
-        def normalise(i):
             nc.gpsimd.tensor_scalar(
                 out=normed[:, i, :],
                 in0=x_sb[:, i, :],
@@ -167,7 +159,7 @@ def tile_swidtblock_pa_kernel(
 
         def transpose_and_scale(half):
             for j in range(CHUNKS):
-                turned = psum.tile([P, HALF_TOKENS], F32, tag="bank")
+                turned = psum.tile([P, HALF_TOKENS], F32, tag="turned")
                 for s in range(HALF_TILES):
                     nc.tensor.transpose(
                         turned[:, P * s : P * (s + 1)],
@@ -182,28 +174,26 @@ def tile_swidtblock_pa_kernel(
                     scale=norm_cols[:, j : j + 1],
                 )
 
-        def regroup_h(half, g):
-            grouped_h = h_stage.tile([P, HALF_TOKENS, PACK], BF16, align_bytes=64)
-            regroup(
-                nc.vector.tensor_copy, grouped_h[:], h_rows[:, half, PACK * g : PACK * (g + 1), :]
-            )
-            return grouped_h
-
-        def quantise_h(half, g, grouped_h):
+        def quantise_h(half):
             tokens = slice(HALF_TOKENS * half, HALF_TOKENS * (half + 1))
-            nc.vector.quantize_mx(
-                out=h_codes[:, g, tokens].bitcast(FP8X4),
-                scales=h_scales[:, g, tokens],
-                in_=grouped_h[:].rearrange("p r t -> p (r t)"),
-            )
+            for g in range(PASSES):
+                grouped_h = h_stage.tile([P, HALF_TOKENS, PACK], BF16, align_bytes=64)
+                regroup(nc.vector.tensor_copy, grouped_h[:], h_rows[:, half, PACK * g : PACK * (g + 1), :])
+                nc.vector.quantize_mx(
+                    out=h_codes[:, g, tokens].bitcast(FP8X4),
+                    scales=h_scales[:, g, tokens],
+                    in_=grouped_h[:].rearrange("p r t -> p (r t)"),
+                )
 
         w_codes = keep.tile([P, PASSES, BLOCKS * N_BLOCK], U32, align_bytes=64)
         w_scales = keep.tile([P, PASSES, BLOCKS * N_BLOCK], U8, align_bytes=64)
 
-        def regroup_w(copy, b, g):
+        def regroup_w(b, g):
             w, part = divmod(b, BLOCKS_PER_WEIGHT)
             grouped_w = w_stage.tile([P, N_BLOCK, PACK], BF16, align_bytes=64)
-            regroup(copy, grouped_w[:], w_raw[:, w, g, :, N_BLOCK * part : N_BLOCK * (part + 1)])
+            regroup(
+                nc.scalar.copy, grouped_w[:], w_raw[:, w, g, :, N_BLOCK * part : N_BLOCK * (part + 1)]
+            )
             return grouped_w
 
         def quantise_w(b, g, grouped_w):
@@ -218,7 +208,7 @@ def tile_swidtblock_pa_kernel(
             w, part = divmod(b, BLOCKS_PER_WEIGHT)
             cols = slice(N_BLOCK * b, N_BLOCK * (b + 1))
             tokens = slice(P * i, P * (i + 1))
-            acc = psum.tile([P, N_BLOCK], F32, tag="bank")
+            acc = psum.tile([P, N_BLOCK], F32, tag="acc")
             for g in range(PASSES):
                 nc.tensor.matmul_mx(
                     out=acc[:],
@@ -243,53 +233,23 @@ def tile_swidtblock_pa_kernel(
                 out=outs[w][tokens, N_BLOCK * part : N_BLOCK * (part + 1)], in_=result[:]
             )
 
-        def project_half(b, half):
-            for i in range(HALF_TILES * half, HALF_TILES * (half + 1)):
-                project(b, i)
-
-        for i in range(HALF_TILES):
-            statistics(i)
-        root(0)
-        statistics(HALF_TILES)
-        scale_and_shift(0)
         for i in range(HALF_TILES):
             normalise(i)
-        w00 = regroup_w(nc.scalar.copy, 0, 0)
-        w10 = regroup_w(nc.scalar.copy, 1, 0)
-        for i in range(HALF_TILES + 1, TOKEN_TILES):
-            statistics(i)
-        root(1)
-        w01 = regroup_w(nc.vector.tensor_copy, 0, 1)
-        scale_and_shift(1)
+        first_0 = regroup_w(0, 0)
         for i in range(HALF_TILES, TOKEN_TILES):
             normalise(i)
-        w11 = regroup_w(nc.vector.tensor_copy, 1, 1)
-        quantise_w(0, 0, w00)
-        quantise_w(1, 0, w10)
-        quantise_w(0, 1, w01)
-        quantise_w(1, 1, w11)
         transpose_and_scale(0)
-        h00 = regroup_h(0, 0)
-        quantise_h(0, 0, h00)
-        h01 = regroup_h(0, 1)
+        first_1 = regroup_w(0, 1)
+        quantise_h(0)
+        quantise_w(0, 0, first_0)
+        quantise_w(0, 1, first_1)
         transpose_and_scale(1)
-        quantise_h(0, 1, h01)
-        project_half(0, 0)
-        h10 = regroup_h(1, 0)
-        project_half(1, 0)
-        h11 = regroup_h(1, 1)
-        quantise_h(1, 0, h10)
-        quantise_h(1, 1, h11)
-        w20 = regroup_w(nc.scalar.copy, 2, 0)
-        project_half(0, 1)
-        quantise_w(2, 0, w20)
-        w21 = regroup_w(nc.scalar.copy, 2, 1)
-        project_half(1, 1)
-        quantise_w(2, 1, w21)
-        for b in range(2, BLOCKS):
+        quantise_h(1)
+        for b in range(BLOCKS):
             for g in range(PASSES):
                 if b + 1 < BLOCKS:
-                    grouped_next = regroup_w(nc.scalar.copy, b + 1, g)
-                project_half(b, g)
+                    grouped_next = regroup_w(b + 1, g)
+                for i in range(HALF_TILES * g, HALF_TILES * (g + 1)):
+                    project(b, i)
                 if b + 1 < BLOCKS:
                     quantise_w(b + 1, g, grouped_next)

from contextlib import ExitStack

import concourse.mybir as mybir
from concourse.masks import make_identity

F32 = mybir.dt.float32
BF16 = mybir.dt.bfloat16
U32 = mybir.dt.uint32
U8 = mybir.dt.uint8
FP8X4 = mybir.dt.float8_e4m3fn_x4
ALU = mybir.AluOpType
ACT = mybir.ActivationFunctionType

P = 128
PACK = 4
K_PASS = P * PACK
D = 1024
PASSES = D // K_PASS
CHUNKS = D // P
TOKENS = 1024
TOKEN_TILES = TOKENS // P
HALF_TILES = TOKEN_TILES // 2
HALF_TOKENS = HALF_TILES * P
WIDTH = 1024
N_BLOCK = 512
BLOCKS_PER_WEIGHT = WIDTH // N_BLOCK
BLOCKS = 3 * BLOCKS_PER_WEIGHT
STAT_PIECE = 512
RUN = 4
EPS = 1e-6
SCALAR_SHARE = 4

FLOPS = 2 * TOKENS * D * 3 * WIDTH


def regroup(copy, grouped, rows):
    copy(
        out=grouped.rearrange("p (c i) t -> p c t i", i=RUN),
        in_=rows.rearrange("p t (c i) -> p c t i", i=RUN),
    )


def tile_swidtblock_pa_kernel(
    tc, x, ln1_gain, ln1_bias, wq, bq, wk, bk, wv, bv, out_0, out_1, out_2
):
    nc = tc.nc
    x_rows = x.flatten_outer_dims()
    weights = [wq, wk, wv]
    biases = [bq, bk, bv]
    outs = [o.rearrange("b t h e -> (b t) (h e)") for o in (out_0, out_1, out_2)]

    with ExitStack() as ctx:
        keep = ctx.enter_context(tc.tile_pool(name="keep", bufs=1))
        h_stage = ctx.enter_context(tc.tile_pool(name="h_stage", bufs=2))
        w_stage = ctx.enter_context(tc.tile_pool(name="w_stage", bufs=4))
        o_stage = ctx.enter_context(tc.tile_pool(name="o_stage", bufs=8))
        psum = ctx.enter_context(tc.psum_pool(name="psum", bufs=4))

        ident_f32 = keep.tile([P, P], F32)
        make_identity(nc, ident_f32[:])
        ident_bf = keep.tile([P, P], BF16)
        nc.vector.tensor_copy(out=ident_bf[:], in_=ident_f32[:])
        eps_t = keep.tile([P, 1], F32)
        nc.vector.memset(eps_t[:], EPS)
        warm = keep.tile([P, 1], F32)
        nc.scalar.activation(out=warm[:], in_=eps_t[:], func=ACT.Sqrt)

        norm_rows = keep.tile([P, P], BF16)
        nc.vector.memset(norm_rows[:], 0.0)
        nc.scalar.dma_start(out=norm_rows[0:CHUNKS, :], in_=ln1_gain.rearrange("(r c) -> r c", c=P))
        nc.scalar.dma_start(
            out=norm_rows[CHUNKS : 2 * CHUNKS, :], in_=ln1_bias.rearrange("(r c) -> r c", c=P)
        )
        bias_rows = keep.tile([P, N_BLOCK], BF16)
        nc.vector.memset(bias_rows[:], 0.0)
        for w in range(3):
            nc.scalar.dma_start(
                out=bias_rows[BLOCKS_PER_WEIGHT * w : BLOCKS_PER_WEIGHT * (w + 1), :],
                in_=biases[w].rearrange("(r c) -> r c", c=N_BLOCK),
            )

        x_sb = keep.tile([P, TOKEN_TILES, D], BF16)
        w_raw = keep.tile([P, 3, PASSES, PACK, WIDTH], BF16)

        def load_x(i):
            nc.sync.dma_start(out=x_sb[:, i, :], in_=x_rows[P * i : P * (i + 1), :])

        def load_w(w, g):
            view = weights[w].rearrange("(g t p) n -> g p t n", t=PACK, p=P)
            nc.sync.dma_start(out=w_raw[:, w, g, :, :], in_=view[g])

        for i in range(HALF_TILES):
            load_x(i)
        load_w(0, 0)
        for i in range(HALF_TILES, TOKEN_TILES):
            load_x(i)
        load_w(0, 1)
        for w in range(1, 3):
            for g in range(PASSES):
                load_w(w, g)

        norm_ps = psum.tile([P, N_BLOCK], F32, tag="acc")
        nc.tensor.matmul(
            out=norm_ps[:, 0:P], lhsT=norm_rows[:], rhs=ident_bf[:], start=True, stop=True
        )
        norm_cols = keep.tile([P, 2 * CHUNKS], F32)
        nc.scalar.copy(out=norm_cols[:], in_=norm_ps[:, 0 : 2 * CHUNKS])
        bias_all = keep.tile([P, BLOCKS * N_BLOCK], F32)
        for b in range(BLOCKS):
            bias_ps = psum.tile([P, N_BLOCK], F32, tag="acc")
            nc.tensor.matmul(
                out=bias_ps[:],
                lhsT=ident_bf[:, b : b + 1].to_broadcast([P, P]),
                rhs=bias_rows[:],
                start=True,
                stop=True,
            )
            nc.scalar.copy(out=bias_all[:, N_BLOCK * b : N_BLOCK * (b + 1)], in_=bias_ps[:])

        stats = keep.tile([P, TOKEN_TILES, D // STAT_PIECE, 6], F32)
        mean_var = keep.tile([P, TOKEN_TILES, 2], F32)
        std = keep.tile([P, TOKEN_TILES], F32)
        rstd = keep.tile([P, TOKEN_TILES], F32)
        shift = keep.tile([P, TOKEN_TILES], F32)
        normed = keep.tile([P, TOKEN_TILES, D], F32)

        def normalise(i):
            for c in range(D // STAT_PIECE):
                nc.vector.bn_stats(
                    out=stats[:, i, c, :], in_=x_sb[:, i, STAT_PIECE * c : STAT_PIECE * (c + 1)]
                )
            nc.vector.bn_aggr(
                out=mean_var[:, i, :], in_=stats[:, i, :, :].rearrange("p c s -> p (c s)")
            )
            nc.scalar.activation(
                out=std[:, i : i + 1], in_=mean_var[:, i, 1:2], func=ACT.Sqrt, bias=eps_t[:, 0:1]
            )
            nc.vector.reciprocal(out=rstd[:, i : i + 1], in_=std[:, i : i + 1])
            nc.vector.tensor_scalar(
                out=shift[:, i : i + 1],
                in0=mean_var[:, i, 0:1],
                scalar1=rstd[:, i : i + 1],
                scalar2=-1.0,
                op0=ALU.mult,
                op1=ALU.mult,
            )
            nc.gpsimd.tensor_scalar(
                out=normed[:, i, :],
                in0=x_sb[:, i, :],
                scalar1=rstd[:, i : i + 1],
                scalar2=shift[:, i : i + 1],
                op0=ALU.mult,
                op1=ALU.add,
            )

        h_rows = keep.tile([P, 2, CHUNKS, HALF_TOKENS], BF16)
        h_codes = keep.tile([P, PASSES, TOKENS], U32, align_bytes=64)
        h_scales = keep.tile([P, PASSES, TOKENS], U8, align_bytes=64)

        def transpose_and_scale(half):
            for j in range(CHUNKS):
                turned = psum.tile([P, HALF_TOKENS], F32, tag="turned")
                for s in range(HALF_TILES):
                    nc.tensor.transpose(
                        turned[:, P * s : P * (s + 1)],
                        normed[:, HALF_TILES * half + s, P * j : P * (j + 1)],
                        ident_f32[:],
                    )
                nc.scalar.activation(
                    out=h_rows[:, half, j, :],
                    in_=turned[:],
                    func=ACT.Identity,
                    bias=norm_cols[:, CHUNKS + j : CHUNKS + j + 1],
                    scale=norm_cols[:, j : j + 1],
                )

        def quantise_h(half):
            tokens = slice(HALF_TOKENS * half, HALF_TOKENS * (half + 1))
            for g in range(PASSES):
                grouped_h = h_stage.tile([P, HALF_TOKENS, PACK], BF16, align_bytes=64)
                regroup(nc.vector.tensor_copy, grouped_h[:], h_rows[:, half, PACK * g : PACK * (g + 1), :])
                nc.vector.quantize_mx(
                    out=h_codes[:, g, tokens].bitcast(FP8X4),
                    scales=h_scales[:, g, tokens],
                    in_=grouped_h[:].rearrange("p r t -> p (r t)"),
                )

        w_codes = keep.tile([P, PASSES, BLOCKS * N_BLOCK], U32, align_bytes=64)
        w_scales = keep.tile([P, PASSES, BLOCKS * N_BLOCK], U8, align_bytes=64)

        def regroup_w(b, g):
            w, part = divmod(b, BLOCKS_PER_WEIGHT)
            grouped_w = w_stage.tile([P, N_BLOCK, PACK], BF16, align_bytes=64)
            regroup(
                nc.scalar.copy, grouped_w[:], w_raw[:, w, g, :, N_BLOCK * part : N_BLOCK * (part + 1)]
            )
            return grouped_w

        def quantise_w(b, g, grouped_w):
            cols = slice(N_BLOCK * b, N_BLOCK * (b + 1))
            nc.vector.quantize_mx(
                out=w_codes[:, g, cols].bitcast(FP8X4),
                scales=w_scales[:, g, cols],
                in_=grouped_w[:].rearrange("p c t -> p (c t)"),
            )

        def project(b, i):
            w, part = divmod(b, BLOCKS_PER_WEIGHT)
            cols = slice(N_BLOCK * b, N_BLOCK * (b + 1))
            tokens = slice(P * i, P * (i + 1))
            acc = psum.tile([P, N_BLOCK], F32, tag="acc")
            for g in range(PASSES):
                nc.tensor.matmul_mx(
                    out=acc[:],
                    lhsT=h_codes[:, g, tokens].bitcast(FP8X4),
                    lhsT_scale=h_scales[:, g, tokens],
                    rhs=w_codes[:, g, cols].bitcast(FP8X4),
                    rhs_scale=w_scales[:, g, cols],
                    start=(g == 0),
                    stop=(g == PASSES - 1),
                )
            result = o_stage.tile([P, N_BLOCK], F32)
            if i % SCALAR_SHARE == SCALAR_SHARE - 1:
                nc.scalar.copy(out=result[:], in_=acc[:])
                nc.gpsimd.tensor_tensor(
                    out=result[:], in0=result[:], in1=bias_all[:, cols], op=ALU.add
                )
            else:
                nc.vector.tensor_tensor(
                    out=result[:], in0=acc[:], in1=bias_all[:, cols], op=ALU.add
                )
            nc.sync.dma_start(
                out=outs[w][tokens, N_BLOCK * part : N_BLOCK * (part + 1)], in_=result[:]
            )

        for i in range(HALF_TILES):
            normalise(i)
        first_0 = regroup_w(0, 0)
        for i in range(HALF_TILES, TOKEN_TILES):
            normalise(i)
        transpose_and_scale(0)
        first_1 = regroup_w(0, 1)
        quantise_h(0)
        quantise_w(0, 0, first_0)
        quantise_w(0, 1, first_1)
        transpose_and_scale(1)
        quantise_h(1)
        for b in range(BLOCKS):
            for g in range(PASSES):
                if b + 1 < BLOCKS:
                    grouped_next = regroup_w(b + 1, g)
                for i in range(HALF_TILES * g, HALF_TILES * (g + 1)):
                    project(b, i)
                if b + 1 < BLOCKS:
                    quantise_w(b + 1, g, grouped_next)
